import numpy as np
import ml_dtypes


def mxq(x, axis, fmt="e4m3"):
    dtype, down = {"e4m3": (ml_dtypes.float8_e4m3fn, 7), "e5m2": (ml_dtypes.float8_e5m2, 14)}[fmt]
    v = np.moveaxis(np.asarray(x, np.float32).astype(ml_dtypes.bfloat16).astype(np.float64), axis, -1)
    blocks = v.reshape(v.shape[:-1] + (-1, 32))
    amax = np.abs(blocks).max(-1, keepdims=True)
    byte = np.maximum(np.where(amax > 0, np.frexp(amax)[1] - 1 + 127, 0) - down, 1)
    scale = np.exp2(byte - 127.0)
    codes = (blocks / scale).astype(np.float32).astype(dtype).astype(np.float64)
    return np.moveaxis((codes * scale).reshape(v.shape), -1, axis)


WIDE = False


def mx_kscale(k):
    if not WIDE:
        return np.ones(k)
    levels = np.array([20, -20, 10, -10, 0])
    a = np.random.permutation(np.resize(levels, k // 512 * 4)).reshape(k // 512, 4)
    idx = np.arange(k)
    return np.exp2(a[idx // 512, idx % 128 // 32])


BF16 = ml_dtypes.bfloat16


def bf(x):
    return np.asarray(x, np.float32).astype(BF16)


def f64(x):
    return np.asarray(x).astype(np.float64)


B, S, H, A, NH = 4, 128, 1536, 1536, 12
HD = A // NH
T = B * S
LN_EPS = 1e-5


def merge_heads(c):
    return c.transpose(0, 2, 1, 3).reshape(B, S, A)


def setup_inputs():
    s = mx_kscale(T).reshape(B, S)
    c0 = bf(np.random.standard_normal((B, NH, S, HD)))
    Wo = bf(np.random.standard_normal((H, A)) / np.sqrt(A))
    bo = bf(np.random.standard_normal(H) * 0.3)
    features = bf(np.random.standard_normal((B, S, H)))
    ln_g = bf(1.0 + 0.1 * np.random.standard_normal(H))
    ln_b = bf(0.2 * np.random.standard_normal(H))
    g = bf(np.random.standard_normal((B, S, H)) * np.exp2(np.random.randint(-12, 1, (B, S, 1))) / s[:, :, None])
    y = merge_heads(f64(c0)) @ f64(Wo).T + f64(bo) + f64(features)
    mu = y.mean(-1, keepdims=True)
    rstd = 1.0 / np.sqrt(y.var(-1, keepdims=True) + LN_EPS)
    return {"ctx_heads": bf(f64(c0) * s[:, None, :, None]),
            "Wo": Wo, "bo": bo, "features": features, "ln_g": ln_g, "ln_b": ln_b,
            "y": np.asarray(y, np.float32),
            "mu": np.asarray(mu, np.float32),
            "rstd": np.asarray(rstd, np.float32),
            "grad_out": g}


def reference(ctx_heads, Wo, bo, features, ln_g, ln_b, y, mu, rstd, grad_out):
    ctx = merge_heads(f64(ctx_heads)).reshape(T, A)
    r = f64(rstd).reshape(T, 1)
    xhat = (f64(y).reshape(T, H) - f64(mu).reshape(T, 1)) * r
    gh = f64(grad_out).reshape(T, H) * f64(ln_g)
    m1 = gh.mean(-1, keepdims=True)
    m2 = (gh * xhat).mean(-1, keepdims=True)
    dy = r * (gh - m1 - xhat * m2)
    return mxq(dy, 0, "e5m2").T @ mxq(ctx, 0, "e4m3")

@@ -1,0 +1,180 @@
+from contextlib import ExitStack
+
+import concourse.mybir as mybir
+
+F32 = mybir.dt.float32
+BF16 = mybir.dt.bfloat16
+U32 = mybir.dt.uint32
+U8 = mybir.dt.uint8
+E4M3_X4 = mybir.dt.float8_e4m3fn_x4
+E5M2_X4 = mybir.dt.float8_e5m2_x4
+ALU = mybir.AluOpType
+ACT = mybir.ActivationFunctionType
+
+P = 128
+PACK = 4
+BATCH = 4
+HEADS = 12
+SEQ = 128
+HEAD_DIM = 128
+FEATURES = 1536
+CTX_COLS = HEADS * HEAD_DIM
+M_TILE = 128
+N_TILE = 512
+M_TILES = FEATURES // M_TILE
+N_TILES = CTX_COLS // N_TILE
+
+FLOPS = 2 * BATCH * SEQ * FEATURES * CTX_COLS
+BYTES = (
+    2 * BATCH * SEQ * CTX_COLS
+    + 2 * BATCH * SEQ * FEATURES
+    + 4 * BATCH * SEQ * FEATURES
+    + 2 * FEATURES
+    + 2 * 4 * BATCH * SEQ
+    + 4 * FEATURES * CTX_COLS
+)
+
+
+def tile_hierarchicalattention_pb_v_kernel(
+    tc, ctx_heads, Wo, bo, features, ln_g, ln_b, y, mu, rstd, grad_out, out
+):
+    nc = tc.nc
+    assert BATCH == PACK and SEQ == P
+
+    with ExitStack() as stack:
+        keep = stack.enter_context(tc.tile_pool(name="keep", bufs=1))
+        results = stack.enter_context(tc.tile_pool(name="results", bufs=4))
+        psum = stack.enter_context(tc.psum_pool(name="psum", bufs=8))
+
+        gain_row = keep.tile([P, FEATURES], BF16)
+        nc.vector.memset(gain_row[:], 0.0)
+        ones = keep.tile([P, P], BF16)
+        nc.vector.memset(ones[:], 1.0)
+        nc.scalar.dma_start(out=gain_row[0:1, :], in_=ln_g.rearrange("(o h) -> o h", o=1))
+
+        rstd_sb = keep.tile([P, PACK], F32)
+        mu_sb = keep.tile([P, PACK], F32)
+        with nc.allow_non_contiguous_dma(reason="512 single float32 values, one per token"):
+            nc.scalar.dma_start(out=rstd_sb[:], in_=rstd.rearrange("b s o -> s (b o)"))
+            nc.scalar.dma_start(out=mu_sb[:], in_=mu.rearrange("b s o -> s (b o)"))
+
+        g_sb = [keep.tile([P, FEATURES], BF16, name="g_sb%d" % b) for b in range(BATCH)]
+        y_sb = [keep.tile([P, FEATURES], F32, name="y_sb%d" % b) for b in range(BATCH)]
+        ctx_raw = keep.tile([P, PACK, CTX_COLS], BF16)
+        for b in range(BATCH):
+            nc.sync.dma_start(out=g_sb[b][:], in_=grad_out[b])
+        for b in range(BATCH):
+            nc.sync.dma_start(
+                out=ctx_raw[:, b, :].rearrange("s (h d) -> s h d", h=HEADS),
+                in_=ctx_heads[b].rearrange("h s d -> s h d"),
+            )
+        for b in range(BATCH):
+            nc.sync.dma_start(out=y_sb[b][:], in_=y[b])
+
+        gain = keep.tile([P, FEATURES], BF16)
+        for n in range(FEATURES // N_TILE):
+            cols = slice(n * N_TILE, (n + 1) * N_TILE)
+            bank = psum.tile([P, N_TILE], F32)
+            nc.tensor.matmul(out=bank[:], lhsT=ones[:], rhs=gain_row[:, cols], start=True, stop=True)
+            nc.scalar.copy(out=gain[:, cols], in_=bank[:])
+
+        neg_r2_mean = keep.tile([P, PACK], F32)
+        nc.vector.scalar_tensor_tensor(
+            out=neg_r2_mean[:], in0=rstd_sb[:], scalar=-1.0 / FEATURES, in1=rstd_sb[:],
+            op0=ALU.mult, op1=ALU.mult,
+        )
+        mu_r2_mean = keep.tile([P, PACK], F32)
+        nc.vector.scalar_tensor_tensor(
+            out=mu_r2_mean[:], in0=neg_r2_mean[:], scalar=-1.0, in1=mu_sb[:],
+            op0=ALU.mult, op1=ALU.mult,
+        )
+
+        ghr = keep.tile([P, PACK, FEATURES], F32)
+        products = keep.tile([P, PACK, FEATURES], F32)
+        line = keep.tile([P, PACK, FEATURES], F32)
+        sum_ghr = keep.tile([P, PACK], F32)
+        sum_products = keep.tile([P, PACK], F32)
+        neg_mean_ghr = keep.tile([P, PACK], F32)
+        slope = keep.tile([P, PACK], F32)
+        shift = keep.tile([P, PACK], F32)
+
+        for b in range(BATCH):
+            tok = slice(b, b + 1)
+            nc.vector.scalar_tensor_tensor(
+                out=ghr[:, b, :], in0=g_sb[b][:], scalar=rstd_sb[:, tok], in1=gain[:],
+                op0=ALU.mult, op1=ALU.mult, accum_out=sum_ghr[:, tok],
+            )
+            nc.vector.tensor_scalar(
+                out=neg_mean_ghr[:, tok], in0=sum_ghr[:, tok], scalar1=-1.0 / FEATURES,
+                scalar2=None, op0=ALU.mult,
+            )
+
+        ctx_grouped = keep.tile([P, CTX_COLS, PACK], BF16, align_bytes=64)
+        ctx_codes = keep.tile([P, CTX_COLS], U32, align_bytes=64)
+        ctx_scales = keep.tile([P, CTX_COLS], U8, align_bytes=64)
+        for n in range(N_TILES):
+            cols = slice(n * N_TILE, (n + 1) * N_TILE)
+            nc.scalar.copy(
+                out=ctx_grouped[:, cols, :], in_=ctx_raw[:, :, cols].rearrange("p b w -> p w b")
+            )
+        for n in range(N_TILES):
+            cols = slice(n * N_TILE, (n + 1) * N_TILE)
+            nc.vector.quantize_mx(
+                out=ctx_codes[:, cols].bitcast(E4M3_X4),
+                scales=ctx_scales[:, cols],
+                in_=ctx_grouped[:, cols, :].rearrange("p w b -> p (w b)"),
+            )
+
+        for b in range(BATCH):
+            tok = slice(b, b + 1)
+            nc.vector.scalar_tensor_tensor(
+                out=products[:, b, :], in0=y_sb[b][:], scalar=mu_sb[:, tok], in1=ghr[:, b, :],
+                op0=ALU.subtract, op1=ALU.mult, accum_out=sum_products[:, tok],
+            )
+            nc.vector.tensor_scalar(
+                out=slope[:, tok], in0=sum_products[:, tok], scalar1=neg_r2_mean[:, tok],
+                scalar2=None, op0=ALU.mult,
+            )
+            nc.vector.tensor_scalar(
+                out=shift[:, tok], in0=sum_products[:, tok], scalar1=mu_r2_mean[:, tok],
+                scalar2=neg_mean_ghr[:, tok], op0=ALU.mult, op1=ALU.add,
+            )
+            nc.scalar.activation(
+                out=line[:, b, :], in_=y_sb[b][:], func=ACT.Identity,
+                bias=shift[:, tok], scale=slope[:, tok],
+            )
+
+        dy_grouped = keep.tile([P, FEATURES, PACK], BF16, align_bytes=64)
+        dy_codes = keep.tile([P, FEATURES], U32, align_bytes=64)
+        dy_scales = keep.tile([P, FEATURES], U8, align_bytes=64)
+        for m in range(M_TILES):
+            rows = slice(m * M_TILE, (m + 1) * M_TILE)
+            nc.vector.tensor_tensor(
+                out=dy_grouped[:, rows, :],
+                in0=ghr[:, :, rows].rearrange("p b w -> p w b"),
+                in1=line[:, :, rows].rearrange("p b w -> p w b"),
+                op=ALU.add,
+            )
+            nc.vector.quantize_mx(
+                out=dy_codes[:, rows].bitcast(E5M2_X4),
+                scales=dy_scales[:, rows],
+                in_=dy_grouped[:, rows, :].rearrange("p w b -> p (w b)"),
+            )
+            result = results.tile([P, CTX_COLS], F32)
+            for n in range(N_TILES):
+                cols = slice(n * N_TILE, (n + 1) * N_TILE)
+                bank = psum.tile([P, N_TILE], F32)
+                nc.tensor.matmul_mx(
+                    out=bank[:],
+                    lhsT=dy_codes[:, rows].bitcast(E5M2_X4),
+                    lhsT_scale=dy_scales[:, rows],
+                    rhs=ctx_codes[:, cols].bitcast(E4M3_X4),
+                    rhs_scale=ctx_scales[:, cols],
+                    start=True,
+                    stop=True,
+                )
+                if n < N_TILES - 1:
+                    nc.scalar.copy(out=result[:, cols], in_=bank[:])
+                else:
+                    nc.vector.tensor_copy(out=result[:, cols], in_=bank[:])
+            nc.sync.dma_start(out=out[rows, :], in_=result[:])

@@ -23,6 +23,8 @@ M_TILE = 128
 N_TILE = 512
 M_TILES = FEATURES // M_TILE
 N_TILES = CTX_COLS // N_TILE
+HEADS_PER_N_TILE = N_TILE // HEAD_DIM
+RUN = 4
 
 FLOPS = 2 * BATCH * SEQ * FEATURES * CTX_COLS
 BYTES = (
@@ -35,22 +37,32 @@ BYTES = (
 )
 
 
+def by_batch(planes):
+    return planes.rearrange("p b (c i) -> p c b i", i=RUN)
+
+
+def by_column(grouped):
+    return grouped.rearrange("p (c i) b -> p c b i", i=RUN)
+
+
 def tile_hierarchicalattention_pb_v_kernel(
     tc, ctx_heads, Wo, bo, features, ln_g, ln_b, y, mu, rstd, grad_out, out
 ):
     nc = tc.nc
     assert BATCH == PACK and SEQ == P
+    assert N_TILES == BATCH - 1
 
     with ExitStack() as stack:
         keep = stack.enter_context(tc.tile_pool(name="keep", bufs=1))
         results = stack.enter_context(tc.tile_pool(name="results", bufs=4))
         psum = stack.enter_context(tc.psum_pool(name="psum", bufs=8))
+        stack.enter_context(tc.manual_schedule())
 
         gain_row = keep.tile([P, FEATURES], BF16)
         nc.vector.memset(gain_row[:], 0.0)
         ones = keep.tile([P, P], BF16)
         nc.vector.memset(ones[:], 1.0)
-        nc.scalar.dma_start(out=gain_row[0:1, :], in_=ln_g.rearrange("(o h) -> o h", o=1))
+        nc.sync.dma_start(out=gain_row[0:1, :], in_=ln_g.rearrange("(o h) -> o h", o=1))
 
         rstd_sb = keep.tile([P, PACK], F32)
         mu_sb = keep.tile([P, PACK], F32)
@@ -60,23 +72,28 @@ def tile_hierarchicalattention_pb_v_kernel(
 
         g_sb = [keep.tile([P, FEATURES], BF16, name="g_sb%d" % b) for b in range(BATCH)]
         y_sb = [keep.tile([P, FEATURES], F32, name="y_sb%d" % b) for b in range(BATCH)]
-        ctx_raw = keep.tile([P, PACK, CTX_COLS], BF16)
+        ctx_raw = [keep.tile([P, PACK, N_TILE], BF16, name="ctx_raw%d" % n) for n in range(N_TILES)]
+
+        def load_ctx(n):
+            heads = slice(n * HEADS_PER_N_TILE, (n + 1) * HEADS_PER_N_TILE)
+            for b in range(BATCH):
+                nc.sync.dma_start(
+                    out=ctx_raw[n][:, b, :].rearrange("s (h d) -> s h d", d=HEAD_DIM),
+                    in_=ctx_heads[b, heads].rearrange("h s d -> s h d"),
+                )
+
         for b in range(BATCH):
             nc.sync.dma_start(out=g_sb[b][:], in_=grad_out[b])
-        for b in range(BATCH):
-            nc.sync.dma_start(
-                out=ctx_raw[:, b, :].rearrange("s (h d) -> s h d", h=HEADS),
-                in_=ctx_heads[b].rearrange("h s d -> s h d"),
-            )
-        for b in range(BATCH):
             nc.sync.dma_start(out=y_sb[b][:], in_=y[b])
+            if b < BATCH - 1:
+                load_ctx(b)
 
         gain = keep.tile([P, FEATURES], BF16)
         for n in range(FEATURES // N_TILE):
             cols = slice(n * N_TILE, (n + 1) * N_TILE)
             bank = psum.tile([P, N_TILE], F32)
             nc.tensor.matmul(out=bank[:], lhsT=ones[:], rhs=gain_row[:, cols], start=True, stop=True)
-            nc.scalar.copy(out=gain[:, cols], in_=bank[:])
+            nc.vector.tensor_copy(out=gain[:, cols], in_=bank[:])
 
         neg_r2_mean = keep.tile([P, PACK], F32)
         nc.vector.scalar_tensor_tensor(
@@ -97,39 +114,27 @@ def tile_hierarchicalattention_pb_v_kernel(
         neg_mean_ghr = keep.tile([P, PACK], F32)
         slope = keep.tile([P, PACK], F32)
         shift = keep.tile([P, PACK], F32)
-
-        for b in range(BATCH):
-            tok = slice(b, b + 1)
-            nc.vector.scalar_tensor_tensor(
-                out=ghr[:, b, :], in0=g_sb[b][:], scalar=rstd_sb[:, tok], in1=gain[:],
-                op0=ALU.mult, op1=ALU.mult, accum_out=sum_ghr[:, tok],
-            )
-            nc.vector.tensor_scalar(
-                out=neg_mean_ghr[:, tok], in0=sum_ghr[:, tok], scalar1=-1.0 / FEATURES,
-                scalar2=None, op0=ALU.mult,
-            )
-
         ctx_grouped = keep.tile([P, CTX_COLS, PACK], BF16, align_bytes=64)
         ctx_codes = keep.tile([P, CTX_COLS], U32, align_bytes=64)
         ctx_scales = keep.tile([P, CTX_COLS], U8, align_bytes=64)
-        for n in range(N_TILES):
-            cols = slice(n * N_TILE, (n + 1) * N_TILE)
-            nc.scalar.copy(
-                out=ctx_grouped[:, cols, :], in_=ctx_raw[:, :, cols].rearrange("p b w -> p w b")
-            )
-        for n in range(N_TILES):
-            cols = slice(n * N_TILE, (n + 1) * N_TILE)
-            nc.vector.quantize_mx(
-                out=ctx_codes[:, cols].bitcast(E4M3_X4),
-                scales=ctx_scales[:, cols],
-                in_=ctx_grouped[:, cols, :].rearrange("p w b -> p (w b)"),
+
+        def scale_grad(b):
+            nc.vector.scalar_tensor_tensor(
+                out=ghr[:, b, :], in0=g_sb[b][:], scalar=rstd_sb[:, b : b + 1], in1=gain[:],
+                op0=ALU.mult, op1=ALU.mult, accum_out=sum_ghr[:, b : b + 1],
             )
 
-        for b in range(BATCH):
-            tok = slice(b, b + 1)
+        def sum_of_products(b):
             nc.vector.scalar_tensor_tensor(
-                out=products[:, b, :], in0=y_sb[b][:], scalar=mu_sb[:, tok], in1=ghr[:, b, :],
-                op0=ALU.subtract, op1=ALU.mult, accum_out=sum_products[:, tok],
+                out=products[:, b, :], in0=y_sb[b][:], scalar=mu_sb[:, b : b + 1], in1=ghr[:, b, :],
+                op0=ALU.subtract, op1=ALU.mult, accum_out=sum_products[:, b : b + 1],
+            )
+
+        def slope_and_shift(b):
+            tok = slice(b, b + 1)
+            nc.vector.tensor_scalar(
+                out=neg_mean_ghr[:, tok], in0=sum_ghr[:, tok], scalar1=-1.0 / FEATURES,
+                scalar2=None, op0=ALU.mult,
             )
             nc.vector.tensor_scalar(
                 out=slope[:, tok], in0=sum_products[:, tok], scalar1=neg_r2_mean[:, tok],
@@ -139,28 +144,73 @@ def tile_hierarchicalattention_pb_v_kernel(
                 out=shift[:, tok], in0=sum_products[:, tok], scalar1=mu_r2_mean[:, tok],
                 scalar2=neg_mean_ghr[:, tok], op0=ALU.mult, op1=ALU.add,
             )
+
+        def draw_line(b, cols):
             nc.scalar.activation(
-                out=line[:, b, :], in_=y_sb[b][:], func=ACT.Identity,
-                bias=shift[:, tok], scale=slope[:, tok],
+                out=line[:, b, cols], in_=y_sb[b][:, cols], func=ACT.Identity,
+                bias=shift[:, b : b + 1], scale=slope[:, b : b + 1],
             )
+
+        def draw_line_on_vector(b, cols):
+            nc.vector.tensor_scalar(
+                out=line[:, b, cols], in0=y_sb[b][:, cols], scalar1=slope[:, b : b + 1],
+                scalar2=shift[:, b : b + 1], op0=ALU.mult, op1=ALU.add,
+            )
+
+        def regroup_ctx(n):
+            cols = slice(n * N_TILE, (n + 1) * N_TILE)
+            nc.scalar.copy(out=by_column(ctx_grouped[:, cols, :]), in_=by_batch(ctx_raw[n][:]))
+
+        def quantise_ctx(n):
+            cols = slice(n * N_TILE, (n + 1) * N_TILE)
+            nc.vector.quantize_mx(
+                out=ctx_codes[:, cols].bitcast(E4M3_X4),
+                scales=ctx_scales[:, cols],
+                in_=ctx_grouped[:, cols, :].rearrange("p w b -> p (w b)"),
+            )
+
+        scale_grad(0)
+        for b in range(BATCH - 1):
+            sum_of_products(b)
+            scale_grad(b + 1)
+            slope_and_shift(b)
+            regroup_ctx(b)
+            draw_line(b, slice(0, FEATURES))
+            quantise_ctx(b)
+        last = BATCH - 1
+        sum_of_products(last)
+        slope_and_shift(last)
+        draw_line_on_vector(last, slice(0, N_TILE))
+        draw_line(last, slice(N_TILE, 2 * N_TILE))
+        draw_line(last, slice(2 * N_TILE, FEATURES))
 
         dy_grouped = keep.tile([P, FEATURES, PACK], BF16, align_bytes=64)
         dy_codes = keep.tile([P, FEATURES], U32, align_bytes=64)
         dy_scales = keep.tile([P, FEATURES], U8, align_bytes=64)
-        for m in range(M_TILES):
+
+        def add_dy(m):
             rows = slice(m * M_TILE, (m + 1) * M_TILE)
             nc.vector.tensor_tensor(
-                out=dy_grouped[:, rows, :],
-                in0=ghr[:, :, rows].rearrange("p b w -> p w b"),
-                in1=line[:, :, rows].rearrange("p b w -> p w b"),
+                out=by_column(dy_grouped[:, rows, :]),
+                in0=by_batch(ghr[:, :, rows]),
+                in1=by_batch(line[:, :, rows]),
                 op=ALU.add,
             )
+
+        def quantise_dy(m):
+            rows = slice(m * M_TILE, (m + 1) * M_TILE)
             nc.vector.quantize_mx(
                 out=dy_codes[:, rows].bitcast(E5M2_X4),
                 scales=dy_scales[:, rows],
                 in_=dy_grouped[:, rows, :].rearrange("p w b -> p (w b)"),
             )
-            result = results.tile([P, CTX_COLS], F32)
+
+        add_dy(0)
+        quantise_dy(0)
+        add_dy(1)
+        for m in range(M_TILES):
+            rows = slice(m * M_TILE, (m + 1) * M_TILE)
+            banks = []
             for n in range(N_TILES):
                 cols = slice(n * N_TILE, (n + 1) * N_TILE)
                 bank = psum.tile([P, N_TILE], F32)
@@ -173,8 +223,16 @@ def tile_hierarchicalattention_pb_v_kernel(
                     start=True,
                     stop=True,
                 )
+                banks.append(bank)
+            if m + 2 < M_TILES:
+                add_dy(m + 2)
+            if m + 1 < M_TILES:
+                quantise_dy(m + 1)
+            result = results.tile([P, CTX_COLS], F32)
+            for n in range(N_TILES):
+                cols = slice(n * N_TILE, (n + 1) * N_TILE)
                 if n < N_TILES - 1:
-                    nc.scalar.copy(out=result[:, cols], in_=bank[:])
+                    nc.scalar.copy(out=result[:, cols], in_=banks[n][:])
                 else:
-                    nc.vector.tensor_copy(out=result[:, cols], in_=bank[:])
+                    nc.vector.tensor_copy(out=result[:, cols], in_=banks[n][:])
             nc.sync.dma_start(out=out[rows, :], in_=result[:])

@@ -37,12 +37,16 @@ BYTES = (
 )
 
 
-def by_batch(planes):
-    return planes.rearrange("p b (c i) -> p c b i", i=RUN)
+def by_slot(planes):
+    return planes.rearrange("p j (c i) -> p c j i", i=RUN)
 
 
 def by_column(grouped):
-    return grouped.rearrange("p (c i) b -> p c b i", i=RUN)
+    return grouped.rearrange("p (c i) j -> p c j i", i=RUN)
+
+
+def slots_of(x):
+    return x.rearrange("b (q j) h -> j q b h", j=PACK)
 
 
 def tile_hierarchicalattention_pb_v_kernel(
@@ -50,7 +54,7 @@ def tile_hierarchicalattention_pb_v_kernel(
 ):
     nc = tc.nc
     assert BATCH == PACK and SEQ == P
-    assert N_TILES == BATCH - 1
+    assert N_TILES <= PACK
 
     with ExitStack() as stack:
         keep = stack.enter_context(tc.tile_pool(name="keep", bufs=1))
@@ -58,36 +62,39 @@ def tile_hierarchicalattention_pb_v_kernel(
         psum = stack.enter_context(tc.psum_pool(name="psum", bufs=8))
         stack.enter_context(tc.manual_schedule())
 
+        ln_g_sb = keep.tile([1, FEATURES], BF16)
+        nc.sync.dma_start(out=ln_g_sb[:], in_=ln_g.rearrange("(o h) -> o h", o=1))
+
+        rstd_sb = keep.tile([P, PACK], F32)
+        mu_sb = keep.tile([P, PACK], F32)
+        nc.scalar.dma_start(out=rstd_sb[:], in_=rstd.rearrange("b (q j) o -> q b (j o)", j=PACK))
+        nc.scalar.dma_start(out=mu_sb[:], in_=mu.rearrange("b (q j) o -> q b (j o)", j=PACK))
+
+        g_sb = [keep.tile([P, FEATURES], BF16, name="g_sb%d" % b) for b in range(PACK)]
+        y_sb = [keep.tile([P, FEATURES], F32, name="y_sb%d" % b) for b in range(PACK)]
+        ctx_raw = [
+            keep.tile([P, HEADS_PER_N_TILE, PACK, HEAD_DIM], BF16, name="ctx_raw%d" % n)
+            for n in range(N_TILES)
+        ]
+
+        def load_ctx(n):
+            for k in range(HEADS_PER_N_TILE):
+                nc.sync.dma_start(
+                    out=ctx_raw[n][:, k, :, :].rearrange("p j d -> p (j d)"),
+                    in_=ctx_heads[:, n * HEADS_PER_N_TILE + k].rearrange("b (q j) d -> q b (j d)", j=PACK),
+                )
+
+        for b in range(PACK):
+            nc.sync.dma_start(out=g_sb[b][:], in_=slots_of(grad_out)[b])
+            if b < N_TILES:
+                load_ctx(b)
+            nc.sync.dma_start(out=y_sb[b][:], in_=slots_of(y)[b])
+
         gain_row = keep.tile([P, FEATURES], BF16)
         nc.vector.memset(gain_row[:], 0.0)
         ones = keep.tile([P, P], BF16)
         nc.vector.memset(ones[:], 1.0)
-        nc.sync.dma_start(out=gain_row[0:1, :], in_=ln_g.rearrange("(o h) -> o h", o=1))
-
-        rstd_sb = keep.tile([P, PACK], F32)
-        mu_sb = keep.tile([P, PACK], F32)
-        with nc.allow_non_contiguous_dma(reason="512 single float32 values, one per token"):
-            nc.scalar.dma_start(out=rstd_sb[:], in_=rstd.rearrange("b s o -> s (b o)"))
-            nc.scalar.dma_start(out=mu_sb[:], in_=mu.rearrange("b s o -> s (b o)"))
-
-        g_sb = [keep.tile([P, FEATURES], BF16, name="g_sb%d" % b) for b in range(BATCH)]
-        y_sb = [keep.tile([P, FEATURES], F32, name="y_sb%d" % b) for b in range(BATCH)]
-        ctx_raw = [keep.tile([P, PACK, N_TILE], BF16, name="ctx_raw%d" % n) for n in range(N_TILES)]
-
-        def load_ctx(n):
-            heads = slice(n * HEADS_PER_N_TILE, (n + 1) * HEADS_PER_N_TILE)
-            for b in range(BATCH):
-                nc.sync.dma_start(
-                    out=ctx_raw[n][:, b, :].rearrange("s (h d) -> s h d", d=HEAD_DIM),
-                    in_=ctx_heads[b, heads].rearrange("h s d -> s h d"),
-                )
-
-        for b in range(BATCH):
-            nc.sync.dma_start(out=g_sb[b][:], in_=grad_out[b])
-            nc.sync.dma_start(out=y_sb[b][:], in_=y[b])
-            if b < BATCH - 1:
-                load_ctx(b)
-
+        nc.vector.tensor_copy(out=gain_row[0:1, :], in_=ln_g_sb[:])
         gain = keep.tile([P, FEATURES], BF16)
         for n in range(FEATURES // N_TILE):
             cols = slice(n * N_TILE, (n + 1) * N_TILE)
@@ -159,7 +166,10 @@ def tile_hierarchicalattention_pb_v_kernel(
 
         def regroup_ctx(n):
             cols = slice(n * N_TILE, (n + 1) * N_TILE)
-            nc.scalar.copy(out=by_column(ctx_grouped[:, cols, :]), in_=by_batch(ctx_raw[n][:]))
+            nc.scalar.copy(
+                out=ctx_grouped[:, cols, :].rearrange("p (k d) j -> p k d j", d=HEAD_DIM),
+                in_=ctx_raw[n][:].rearrange("p k j d -> p k d j"),
+            )
 
         def quantise_ctx(n):
             cols = slice(n * N_TILE, (n + 1) * N_TILE)
@@ -170,14 +180,16 @@ def tile_hierarchicalattention_pb_v_kernel(
             )
 
         scale_grad(0)
-        for b in range(BATCH - 1):
+        regroup_ctx(0)
+        for b in range(PACK - 1):
             sum_of_products(b)
             scale_grad(b + 1)
             slope_and_shift(b)
-            regroup_ctx(b)
+            if b + 1 < N_TILES:
+                regroup_ctx(b + 1)
             draw_line(b, slice(0, FEATURES))
-            quantise_ctx(b)
-        last = BATCH - 1
+        quantise_ctx(0)
+        last = PACK - 1
         sum_of_products(last)
         slope_and_shift(last)
         draw_line_on_vector(last, slice(0, N_TILE))
@@ -192,8 +204,8 @@ def tile_hierarchicalattention_pb_v_kernel(
             rows = slice(m * M_TILE, (m + 1) * M_TILE)
             nc.vector.tensor_tensor(
                 out=by_column(dy_grouped[:, rows, :]),
-                in0=by_batch(ghr[:, :, rows]),
-                in1=by_batch(line[:, :, rows]),
+                in0=by_slot(ghr[:, :, rows]),
+                in1=by_slot(line[:, :, rows]),
                 op=ALU.add,
             )
 
@@ -207,6 +219,8 @@ def tile_hierarchicalattention_pb_v_kernel(
 
         add_dy(0)
         quantise_dy(0)
+        for n in range(1, N_TILES):
+            quantise_ctx(n)
         add_dy(1)
         for m in range(M_TILES):
             rows = slice(m * M_TILE, (m + 1) * M_TILE)
@@ -231,8 +245,8 @@ def tile_hierarchicalattention_pb_v_kernel(
             result = results.tile([P, CTX_COLS], F32)
             for n in range(N_TILES):
                 cols = slice(n * N_TILE, (n + 1) * N_TILE)
-                if n < N_TILES - 1:
-                    nc.scalar.copy(out=result[:, cols], in_=banks[n][:])
-                else:
+                if (m * N_TILES + n) % 4 == 3:
                     nc.vector.tensor_copy(out=result[:, cols], in_=banks[n][:])
+                else:
+                    nc.scalar.copy(out=result[:, cols], in_=banks[n][:])
             nc.sync.dma_start(out=out[rows, :], in_=result[:])

@@ -96,11 +96,14 @@ def tile_hierarchicalattention_pb_v_kernel(
         nc.vector.memset(ones[:], 1.0)
         nc.vector.tensor_copy(out=gain_row[0:1, :], in_=ln_g_sb[:])
         gain = keep.tile([P, FEATURES], BF16)
+        gain_banks = []
         for n in range(FEATURES // N_TILE):
             cols = slice(n * N_TILE, (n + 1) * N_TILE)
-            bank = psum.tile([P, N_TILE], F32)
-            nc.tensor.matmul(out=bank[:], lhsT=ones[:], rhs=gain_row[:, cols], start=True, stop=True)
-            nc.vector.tensor_copy(out=gain[:, cols], in_=bank[:])
+            gain_bank = psum.tile([P, N_TILE], BF16, tag="bank")
+            nc.tensor.matmul(
+                out=gain_bank[:], lhsT=ones[:], rhs=gain_row[:, cols], start=True, stop=True
+            )
+            gain_banks.append(gain_bank)
 
         neg_r2_mean = keep.tile([P, PACK], F32)
         nc.vector.scalar_tensor_tensor(
@@ -167,8 +170,8 @@ def tile_hierarchicalattention_pb_v_kernel(
         def regroup_ctx(n):
             cols = slice(n * N_TILE, (n + 1) * N_TILE)
             nc.scalar.copy(
-                out=ctx_grouped[:, cols, :].rearrange("p (k d) j -> p k d j", d=HEAD_DIM),
-                in_=ctx_raw[n][:].rearrange("p k j d -> p k d j"),
+                out=ctx_grouped[:, cols, :].rearrange("p (k c i) j -> p k c j i", k=HEADS_PER_N_TILE, i=RUN),
+                in_=ctx_raw[n][:].rearrange("p k j (c i) -> p k c j i", i=RUN),
             )
 
         def quantise_ctx(n):
@@ -179,7 +182,17 @@ def tile_hierarchicalattention_pb_v_kernel(
                 in_=ctx_grouped[:, cols, :].rearrange("p w b -> p (w b)"),
             )
 
-        scale_grad(0)
+        first_sums = keep.tile([P, FEATURES // N_TILE], F32)
+        for n in range(FEATURES // N_TILE):
+            cols = slice(n * N_TILE, (n + 1) * N_TILE)
+            nc.vector.scalar_tensor_tensor(
+                out=ghr[:, 0, cols], in0=g_sb[0][:, cols], scalar=rstd_sb[:, 0:1],
+                in1=gain_banks[n][:], op0=ALU.mult, op1=ALU.mult, accum_out=first_sums[:, n : n + 1],
+            )
+            nc.scalar.copy(out=gain[:, cols], in_=gain_banks[n][:])
+        nc.vector.tensor_reduce(
+            out=sum_ghr[:, 0:1], in_=first_sums[:], axis=mybir.AxisListType.X, op=ALU.add
+        )
         regroup_ctx(0)
         for b in range(PACK - 1):
             sum_of_products(b)

@@ -67,8 +67,8 @@ def tile_hierarchicalattention_pb_v_kernel(
 
         rstd_sb = keep.tile([P, PACK], F32)
         mu_sb = keep.tile([P, PACK], F32)
-        nc.scalar.dma_start(out=rstd_sb[:], in_=rstd.rearrange("b (q j) o -> q b (j o)", j=PACK))
-        nc.scalar.dma_start(out=mu_sb[:], in_=mu.rearrange("b (q j) o -> q b (j o)", j=PACK))
+        nc.sync.dma_start(out=rstd_sb[:], in_=rstd.rearrange("b (q j) o -> q b (j o)", j=PACK))
+        nc.sync.dma_start(out=mu_sb[:], in_=mu.rearrange("b (q j) o -> q b (j o)", j=PACK))
 
         g_sb = [keep.tile([P, FEATURES], BF16, name="g_sb%d" % b) for b in range(PACK)]
         y_sb = [keep.tile([P, FEATURES], F32, name="y_sb%d" % b) for b in range(PACK)]
@@ -105,17 +105,6 @@ def tile_hierarchicalattention_pb_v_kernel(
             )
             gain_banks.append(gain_bank)
 
-        neg_r2_mean = keep.tile([P, PACK], F32)
-        nc.vector.scalar_tensor_tensor(
-            out=neg_r2_mean[:], in0=rstd_sb[:], scalar=-1.0 / FEATURES, in1=rstd_sb[:],
-            op0=ALU.mult, op1=ALU.mult,
-        )
-        mu_r2_mean = keep.tile([P, PACK], F32)
-        nc.vector.scalar_tensor_tensor(
-            out=mu_r2_mean[:], in0=neg_r2_mean[:], scalar=-1.0, in1=mu_sb[:],
-            op0=ALU.mult, op1=ALU.mult,
-        )
-
         ghr = keep.tile([P, PACK, FEATURES], F32)
         products = keep.tile([P, PACK, FEATURES], F32)
         line = keep.tile([P, PACK, FEATURES], F32)
@@ -140,12 +129,15 @@ def tile_hierarchicalattention_pb_v_kernel(
                 op0=ALU.subtract, op1=ALU.mult, accum_out=sum_products[:, b : b + 1],
             )
 
-        def slope_and_shift(b):
+        def mean_of_ghr(b):
             tok = slice(b, b + 1)
             nc.vector.tensor_scalar(
                 out=neg_mean_ghr[:, tok], in0=sum_ghr[:, tok], scalar1=-1.0 / FEATURES,
                 scalar2=None, op0=ALU.mult,
             )
+
+        def slope_and_shift(b):
+            tok = slice(b, b + 1)
             nc.vector.tensor_scalar(
                 out=slope[:, tok], in0=sum_products[:, tok], scalar1=neg_r2_mean[:, tok],
                 scalar2=None, op0=ALU.mult,
@@ -194,8 +186,21 @@ def tile_hierarchicalattention_pb_v_kernel(
             out=sum_ghr[:, 0:1], in_=first_sums[:], axis=mybir.AxisListType.X, op=ALU.add
         )
         regroup_ctx(0)
+
+        neg_r2_mean = keep.tile([P, PACK], F32)
+        nc.vector.scalar_tensor_tensor(
+            out=neg_r2_mean[:], in0=rstd_sb[:], scalar=-1.0 / FEATURES, in1=rstd_sb[:],
+            op0=ALU.mult, op1=ALU.mult,
+        )
+        mu_r2_mean = keep.tile([P, PACK], F32)
+        nc.vector.scalar_tensor_tensor(
+            out=mu_r2_mean[:], in0=neg_r2_mean[:], scalar=-1.0, in1=mu_sb[:],
+            op0=ALU.mult, op1=ALU.mult,
+        )
+
         for b in range(PACK - 1):
             sum_of_products(b)
+            mean_of_ghr(b)
             scale_grad(b + 1)
             slope_and_shift(b)
             if b + 1 < N_TILES:
@@ -203,6 +208,7 @@ def tile_hierarchicalattention_pb_v_kernel(
             draw_line(b, slice(0, FEATURES))
         quantise_ctx(0)
         last = PACK - 1
+        mean_of_ghr(last)
         sum_of_products(last)
         slope_and_shift(last)
         draw_line_on_vector(last, slice(0, N_TILE))

@@ -119,7 +119,7 @@ def tile_hierarchicalattention_pb_v_kernel(
 
         def scale_grad(b):
             nc.vector.scalar_tensor_tensor(
-                out=ghr[:, b, :], in0=g_sb[b][:], scalar=rstd_sb[:, b : b + 1], in1=gain[:],
+                out=ghr[:, b, :], in0=gain[:], scalar=rstd_sb[:, b : b + 1], in1=g_sb[b][:],
                 op0=ALU.mult, op1=ALU.mult, accum_out=sum_ghr[:, b : b + 1],
             )
 
@@ -178,8 +178,8 @@ def tile_hierarchicalattention_pb_v_kernel(
         for n in range(FEATURES // N_TILE):
             cols = slice(n * N_TILE, (n + 1) * N_TILE)
             nc.vector.scalar_tensor_tensor(
-                out=ghr[:, 0, cols], in0=g_sb[0][:, cols], scalar=rstd_sb[:, 0:1],
-                in1=gain_banks[n][:], op0=ALU.mult, op1=ALU.mult, accum_out=first_sums[:, n : n + 1],
+                out=ghr[:, 0, cols], in0=gain_banks[n][:], scalar=rstd_sb[:, 0:1],
+                in1=g_sb[0][:, cols], op0=ALU.mult, op1=ALU.mult, accum_out=first_sums[:, n : n + 1],
             )
             nc.scalar.copy(out=gain[:, cols], in_=gain_banks[n][:])
         nc.vector.tensor_reduce(

@@ -54,7 +54,12 @@ def tile_hierarchicalattention_pb_v_kernel(
 ):
     nc = tc.nc
     assert BATCH == PACK and SEQ == P
-    assert N_TILES <= PACK
+    THIRDS = FEATURES // N_TILE
+    HALF = 2
+    HALVES = HEADS // HALF
+    HALF_COLS = HALF * HEAD_DIM
+    TILES_PER_THIRD = N_TILE // M_TILE
+    HEAD = 2 * M_TILE
 
     with ExitStack() as stack:
         keep = stack.enter_context(tc.tile_pool(name="keep", bufs=1))
@@ -64,41 +69,61 @@ def tile_hierarchicalattention_pb_v_kernel(
 
         ln_g_sb = keep.tile([1, FEATURES], BF16)
         nc.sync.dma_start(out=ln_g_sb[:], in_=ln_g.rearrange("(o h) -> o h", o=1))
-
         rstd_sb = keep.tile([P, PACK], F32)
         mu_sb = keep.tile([P, PACK], F32)
         nc.sync.dma_start(out=rstd_sb[:], in_=rstd.rearrange("b (q j) o -> q b (j o)", j=PACK))
-        nc.sync.dma_start(out=mu_sb[:], in_=mu.rearrange("b (q j) o -> q b (j o)", j=PACK))
 
-        g_sb = [keep.tile([P, FEATURES], BF16, name="g_sb%d" % b) for b in range(PACK)]
-        y_sb = [keep.tile([P, FEATURES], F32, name="y_sb%d" % b) for b in range(PACK)]
+        g_first = [keep.tile([P, N_TILE], BF16, name="g_first%d" % n) for n in range(THIRDS)]
+        g_sb = [keep.tile([P, FEATURES], BF16, name="g_sb%d" % j) for j in range(1, PACK)]
+        y_sb = [keep.tile([P, FEATURES], F32, name="y_sb%d" % j) for j in range(PACK)]
         ctx_raw = [
-            keep.tile([P, HEADS_PER_N_TILE, PACK, HEAD_DIM], BF16, name="ctx_raw%d" % n)
-            for n in range(N_TILES)
+            keep.tile([P, HALF, PACK, HEAD_DIM], BF16, name="ctx_raw%d" % i) for i in range(HALVES)
         ]
 
-        def load_ctx(n):
-            for k in range(HEADS_PER_N_TILE):
+        def load_g(j):
+            if j == 0:
+                for n in range(THIRDS):
+                    nc.sync.dma_start(
+                        out=g_first[n][:], in_=slots_of(grad_out)[0][:, :, n * N_TILE : (n + 1) * N_TILE]
+                    )
+            else:
+                nc.sync.dma_start(out=g_sb[j - 1][:], in_=slots_of(grad_out)[j])
+
+        def load_y(j):
+            nc.sync.dma_start(out=y_sb[j][:], in_=slots_of(y)[j])
+
+        def load_ctx(i):
+            for k in range(HALF):
                 nc.sync.dma_start(
-                    out=ctx_raw[n][:, k, :, :].rearrange("p j d -> p (j d)"),
-                    in_=ctx_heads[:, n * HEADS_PER_N_TILE + k].rearrange("b (q j) d -> q b (j d)", j=PACK),
+                    out=ctx_raw[i][:, k, :, :].rearrange("p j d -> p (j d)"),
+                    in_=ctx_heads[:, i * HALF + k].rearrange("b (q j) d -> q b (j d)", j=PACK),
                 )
 
-        for b in range(PACK):
-            nc.sync.dma_start(out=g_sb[b][:], in_=slots_of(grad_out)[b])
-            if b < N_TILES:
-                load_ctx(b)
-            nc.sync.dma_start(out=y_sb[b][:], in_=slots_of(y)[b])
+        load_g(0)
+        nc.sync.dma_start(out=mu_sb[:], in_=mu.rearrange("b (q j) o -> q b (j o)", j=PACK))
+        load_y(0)
+        load_ctx(0)
+        load_ctx(1)
+        load_g(1)
+        load_y(1)
+        load_ctx(2)
+        load_g(2)
+        load_y(2)
+        load_ctx(3)
+        load_ctx(4)
+        load_g(3)
+        load_ctx(5)
+        load_y(3)
 
         gain_row = keep.tile([P, FEATURES], BF16)
         nc.vector.memset(gain_row[:], 0.0)
         ones = keep.tile([P, P], BF16)
         nc.vector.memset(ones[:], 1.0)
-        nc.vector.tensor_copy(out=gain_row[0:1, :], in_=ln_g_sb[:])
         gain = keep.tile([P, FEATURES], BF16)
         gain_banks = []
-        for n in range(FEATURES // N_TILE):
+        for n in range(THIRDS):
             cols = slice(n * N_TILE, (n + 1) * N_TILE)
+            nc.vector.tensor_copy(out=gain_row[0:1, cols], in_=ln_g_sb[:, cols])
             gain_bank = psum.tile([P, N_TILE], BF16, tag="bank")
             nc.tensor.matmul(
                 out=gain_bank[:], lhsT=ones[:], rhs=gain_row[:, cols], start=True, stop=True
@@ -106,64 +131,68 @@ def tile_hierarchicalattention_pb_v_kernel(
             gain_banks.append(gain_bank)
 
         ghr = keep.tile([P, PACK, FEATURES], F32)
-        products = keep.tile([P, PACK, FEATURES], F32)
-        line = keep.tile([P, PACK, FEATURES], F32)
+        products = keep.tile([P, FEATURES], F32)
+        line = [keep.tile([P, PACK, N_TILE], F32, name="line%d" % c) for c in range(THIRDS)]
         sum_ghr = keep.tile([P, PACK], F32)
         sum_products = keep.tile([P, PACK], F32)
         neg_mean_ghr = keep.tile([P, PACK], F32)
         slope = keep.tile([P, PACK], F32)
         shift = keep.tile([P, PACK], F32)
+        scaled_parts = keep.tile([P, THIRDS], F32)
+        w_head = keep.tile([P, HEAD], F32)
         ctx_grouped = keep.tile([P, CTX_COLS, PACK], BF16, align_bytes=64)
         ctx_codes = keep.tile([P, CTX_COLS], U32, align_bytes=64)
         ctx_scales = keep.tile([P, CTX_COLS], U8, align_bytes=64)
+        dy_grouped = keep.tile([P, FEATURES, PACK], BF16, align_bytes=64)
+        dy_codes = keep.tile([P, FEATURES], U32, align_bytes=64)
+        dy_scales = keep.tile([P, FEATURES], U8, align_bytes=64)
+        last = PACK - 1
 
-        def scale_grad(b):
+        def scale_grad(j):
             nc.vector.scalar_tensor_tensor(
-                out=ghr[:, b, :], in0=gain[:], scalar=rstd_sb[:, b : b + 1], in1=g_sb[b][:],
-                op0=ALU.mult, op1=ALU.mult, accum_out=sum_ghr[:, b : b + 1],
+                out=ghr[:, j, :], in0=gain[:], scalar=rstd_sb[:, j : j + 1], in1=g_sb[j - 1][:],
+                op0=ALU.mult, op1=ALU.mult, accum_out=sum_ghr[:, j : j + 1],
             )
 
-        def sum_of_products(b):
+        def sum_of_products(j):
             nc.vector.scalar_tensor_tensor(
-                out=products[:, b, :], in0=y_sb[b][:], scalar=mu_sb[:, b : b + 1], in1=ghr[:, b, :],
-                op0=ALU.subtract, op1=ALU.mult, accum_out=sum_products[:, b : b + 1],
+                out=products[:], in0=y_sb[j][:], scalar=mu_sb[:, j : j + 1], in1=ghr[:, j, :],
+                op0=ALU.subtract, op1=ALU.mult, accum_out=sum_products[:, j : j + 1],
             )
 
-        def mean_of_ghr(b):
-            tok = slice(b, b + 1)
-            nc.vector.tensor_scalar(
-                out=neg_mean_ghr[:, tok], in0=sum_ghr[:, tok], scalar1=-1.0 / FEATURES,
-                scalar2=None, op0=ALU.mult,
-            )
-
-        def slope_and_shift(b):
-            tok = slice(b, b + 1)
-            nc.vector.tensor_scalar(
-                out=slope[:, tok], in0=sum_products[:, tok], scalar1=neg_r2_mean[:, tok],
-                scalar2=None, op0=ALU.mult,
-            )
-            nc.vector.tensor_scalar(
-                out=shift[:, tok], in0=sum_products[:, tok], scalar1=mu_r2_mean[:, tok],
-                scalar2=neg_mean_ghr[:, tok], op0=ALU.mult, op1=ALU.add,
-            )
-
-        def draw_line(b, cols):
+        def factors_on_scalar(j):
+            tok = slice(j, j + 1)
             nc.scalar.activation(
-                out=line[:, b, cols], in_=y_sb[b][:, cols], func=ACT.Identity,
-                bias=shift[:, b : b + 1], scale=slope[:, b : b + 1],
+                out=slope[:, tok], in_=sum_products[:, tok], func=ACT.Identity, scale=neg_r2_mean[:, tok]
+            )
+            nc.scalar.activation(
+                out=shift[:, tok], in_=sum_products[:, tok], func=ACT.Identity,
+                scale=mu_r2_mean[:, tok], bias=neg_mean_ghr[:, tok],
             )
 
-        def draw_line_on_vector(b, cols):
-            nc.vector.tensor_scalar(
-                out=line[:, b, cols], in0=y_sb[b][:, cols], scalar1=slope[:, b : b + 1],
-                scalar2=shift[:, b : b + 1], op0=ALU.mult, op1=ALU.add,
+        def mean_on_scalar(j):
+            if j == 0:
+                nc.scalar.activation(
+                    out=scaled_parts[:], in_=first_sums[:], func=ACT.Identity, scale=-1.0 / FEATURES,
+                    accum_out=neg_mean_ghr[:, 0:1],
+                )
+            else:
+                nc.scalar.activation(
+                    out=neg_mean_ghr[:, j : j + 1], in_=sum_ghr[:, j : j + 1], func=ACT.Identity,
+                    scale=-1.0 / FEATURES,
+                )
+
+        def draw_line(j, c, lo=0):
+            nc.scalar.activation(
+                out=line[c][:, j, lo:N_TILE], in_=y_sb[j][:, c * N_TILE + lo : (c + 1) * N_TILE],
+                func=ACT.Identity, bias=shift[:, j : j + 1], scale=slope[:, j : j + 1],
             )
 
-        def regroup_ctx(n):
-            cols = slice(n * N_TILE, (n + 1) * N_TILE)
+        def regroup_ctx(i):
+            cols = slice(i * HALF_COLS, (i + 1) * HALF_COLS)
             nc.scalar.copy(
-                out=ctx_grouped[:, cols, :].rearrange("p (k c i) j -> p k c j i", k=HEADS_PER_N_TILE, i=RUN),
-                in_=ctx_raw[n][:].rearrange("p k j (c i) -> p k c j i", i=RUN),
+                out=ctx_grouped[:, cols, :].rearrange("p (k c i) j -> p k c j i", k=HALF, i=RUN),
+                in_=ctx_raw[i][:].rearrange("p k j (c i) -> p k c j i", i=RUN),
             )
 
         def quantise_ctx(n):
@@ -174,57 +203,13 @@ def tile_hierarchicalattention_pb_v_kernel(
                 in_=ctx_grouped[:, cols, :].rearrange("p w b -> p (w b)"),
             )
 
-        first_sums = keep.tile([P, FEATURES // N_TILE], F32)
-        for n in range(FEATURES // N_TILE):
-            cols = slice(n * N_TILE, (n + 1) * N_TILE)
-            nc.vector.scalar_tensor_tensor(
-                out=ghr[:, 0, cols], in0=gain_banks[n][:], scalar=rstd_sb[:, 0:1],
-                in1=g_sb[0][:, cols], op0=ALU.mult, op1=ALU.mult, accum_out=first_sums[:, n : n + 1],
-            )
-            nc.scalar.copy(out=gain[:, cols], in_=gain_banks[n][:])
-        nc.vector.tensor_reduce(
-            out=sum_ghr[:, 0:1], in_=first_sums[:], axis=mybir.AxisListType.X, op=ALU.add
-        )
-        regroup_ctx(0)
-
-        neg_r2_mean = keep.tile([P, PACK], F32)
-        nc.vector.scalar_tensor_tensor(
-            out=neg_r2_mean[:], in0=rstd_sb[:], scalar=-1.0 / FEATURES, in1=rstd_sb[:],
-            op0=ALU.mult, op1=ALU.mult,
-        )
-        mu_r2_mean = keep.tile([P, PACK], F32)
-        nc.vector.scalar_tensor_tensor(
-            out=mu_r2_mean[:], in0=neg_r2_mean[:], scalar=-1.0, in1=mu_sb[:],
-            op0=ALU.mult, op1=ALU.mult,
-        )
-
-        for b in range(PACK - 1):
-            sum_of_products(b)
-            mean_of_ghr(b)
-            scale_grad(b + 1)
-            slope_and_shift(b)
-            if b + 1 < N_TILES:
-                regroup_ctx(b + 1)
-            draw_line(b, slice(0, FEATURES))
-        quantise_ctx(0)
-        last = PACK - 1
-        mean_of_ghr(last)
-        sum_of_products(last)
-        slope_and_shift(last)
-        draw_line_on_vector(last, slice(0, N_TILE))
-        draw_line(last, slice(N_TILE, 2 * N_TILE))
-        draw_line(last, slice(2 * N_TILE, FEATURES))
-
-        dy_grouped = keep.tile([P, FEATURES, PACK], BF16, align_bytes=64)
-        dy_codes = keep.tile([P, FEATURES], U32, align_bytes=64)
-        dy_scales = keep.tile([P, FEATURES], U8, align_bytes=64)
-
         def add_dy(m):
             rows = slice(m * M_TILE, (m + 1) * M_TILE)
+            in_third = slice((m % TILES_PER_THIRD) * M_TILE, (m % TILES_PER_THIRD + 1) * M_TILE)
             nc.vector.tensor_tensor(
                 out=by_column(dy_grouped[:, rows, :]),
                 in0=by_slot(ghr[:, :, rows]),
-                in1=by_slot(line[:, :, rows]),
+                in1=by_slot(line[m // TILES_PER_THIRD][:, :, in_third]),
                 op=ALU.add,
             )
 
@@ -236,17 +221,91 @@ def tile_hierarchicalattention_pb_v_kernel(
                 in_=dy_grouped[:, rows, :].rearrange("p w b -> p (w b)"),
             )
 
+        first_sums = keep.tile([P, THIRDS], F32)
+        for n in range(THIRDS):
+            cols = slice(n * N_TILE, (n + 1) * N_TILE)
+            nc.vector.scalar_tensor_tensor(
+                out=ghr[:, 0, cols], in0=gain_banks[n][:], scalar=rstd_sb[:, 0:1],
+                in1=g_first[n][:], op0=ALU.mult, op1=ALU.mult, accum_out=first_sums[:, n : n + 1],
+            )
+            nc.scalar.copy(out=gain[:, cols], in_=gain_banks[n][:])
+        r2 = keep.tile([P, PACK], F32)
+        r2_mean = keep.tile([P, PACK], F32)
+        neg_r2_mean = keep.tile([P, PACK], F32)
+        mu_r2_mean = keep.tile([P, PACK], F32)
+        nc.gpsimd.tensor_tensor(out=r2[:], in0=rstd_sb[:], in1=rstd_sb[:], op=ALU.mult)
+        nc.gpsimd.tensor_scalar(
+            out=r2_mean[:], in0=r2[:], scalar1=1.0 / FEATURES, scalar2=None, op0=ALU.mult
+        )
+        nc.gpsimd.tensor_scalar(
+            out=neg_r2_mean[:], in0=r2_mean[:], scalar1=-1.0, scalar2=None, op0=ALU.mult
+        )
+        nc.gpsimd.tensor_tensor(out=mu_r2_mean[:], in0=r2_mean[:], in1=mu_sb[:], op=ALU.mult)
+
+        sum_of_products(0)
+        scale_grad(1)
+        regroup_ctx(0)
+        regroup_ctx(1)
+        mean_on_scalar(0)
+        factors_on_scalar(0)
+        draw_line(0, 0)
+        sum_of_products(1)
+        scale_grad(2)
+        regroup_ctx(2)
+        mean_on_scalar(1)
+        factors_on_scalar(1)
+        draw_line(1, 0)
+        draw_line(0, 1)
+        draw_line(0, 2)
+        sum_of_products(2)
+        scale_grad(3)
+        regroup_ctx(3)
+        regroup_ctx(4)
+        mean_on_scalar(2)
+        factors_on_scalar(2)
+        draw_line(2, 0)
+        mean_on_scalar(last)
+        nc.scalar.activation(
+            out=w_head[:], in_=y_sb[last][:, 0:HEAD], func=ACT.Identity,
+            bias=mu_r2_mean[:, last : last + 1], scale=neg_r2_mean[:, last : last + 1],
+        )
+        regroup_ctx(5)
+        draw_line(1, 1)
+        draw_line(1, 2)
+        quantise_ctx(0)
+        sum_of_products(last)
+        nc.vector.tensor_scalar(
+            out=line[0][:, last, 0:HEAD], in0=w_head[:], scalar1=sum_products[:, last : last + 1],
+            scalar2=neg_mean_ghr[:, last : last + 1], op0=ALU.mult, op1=ALU.add,
+        )
+        factors_on_scalar(last)
+        draw_line(last, 0, HEAD)
+        draw_line(last - 1, 1)
+        draw_line(last, 1)
+
+        def draw_late(m):
+            if m == 2 * TILES_PER_THIRD:
+                c = m // TILES_PER_THIRD
+                for j in (last - 1, last):
+                    nc.vector.tensor_scalar(
+                        out=line[c][:, j, :], in0=y_sb[j][:, c * N_TILE : (c + 1) * N_TILE],
+                        scalar1=slope[:, j : j + 1], scalar2=shift[:, j : j + 1],
+                        op0=ALU.mult, op1=ALU.add,
+                    )
+
         add_dy(0)
         quantise_dy(0)
-        for n in range(1, N_TILES):
-            quantise_ctx(n)
+        quantise_ctx(1)
         add_dy(1)
+        quantise_ctx(2)
+        quantise_dy(1)
+        add_dy(2)
         for m in range(M_TILES):
             rows = slice(m * M_TILE, (m + 1) * M_TILE)
             banks = []
             for n in range(N_TILES):
                 cols = slice(n * N_TILE, (n + 1) * N_TILE)
-                bank = psum.tile([P, N_TILE], F32)
+                bank = psum.tile([P, N_TILE], F32, tag="bank")
                 nc.tensor.matmul_mx(
                     out=bank[:],
                     lhsT=dy_codes[:, rows].bitcast(E5M2_X4),
@@ -257,15 +316,19 @@ def tile_hierarchicalattention_pb_v_kernel(
                     stop=True,
                 )
                 banks.append(bank)
+            draw_late(m + 4)
             if m + 2 < M_TILES:
-                add_dy(m + 2)
-            if m + 1 < M_TILES:
-                quantise_dy(m + 1)
+                quantise_dy(m + 2)
+            if m + 3 < M_TILES:
+                add_dy(m + 3)
             result = results.tile([P, CTX_COLS], F32)
             for n in range(N_TILES):
                 cols = slice(n * N_TILE, (n + 1) * N_TILE)
-                if (m * N_TILES + n) % 4 == 3:
+                if n == N_TILES - 1 and m > 3:
                     nc.vector.tensor_copy(out=result[:, cols], in_=banks[n][:])
                 else:
                     nc.scalar.copy(out=result[:, cols], in_=banks[n][:])
-            nc.sync.dma_start(out=out[rows, :], in_=result[:])
+                if m <= 3:
+                    nc.sync.dma_start(out=out[rows, cols], in_=result[:, cols])
+            if m > 3:
+                nc.sync.dma_start(out=out[rows, :], in_=result[:])

@@ -103,17 +103,17 @@ def tile_hierarchicalattention_pb_v_kernel(
         nc.sync.dma_start(out=mu_sb[:], in_=mu.rearrange("b (q j) o -> q b (j o)", j=PACK))
         load_y(0)
         load_ctx(0)
-        load_ctx(1)
         load_g(1)
+        load_ctx(1)
+        load_g(2)
         load_y(1)
         load_ctx(2)
-        load_g(2)
+        load_g(3)
         load_y(2)
         load_ctx(3)
         load_ctx(4)
-        load_g(3)
-        load_ctx(5)
         load_y(3)
+        load_ctx(5)
 
         gain_row = keep.tile([P, FEATURES], BF16)
         nc.vector.memset(gain_row[:], 0.0)
@@ -138,7 +138,8 @@ def tile_hierarchicalattention_pb_v_kernel(
         neg_mean_ghr = keep.tile([P, PACK], F32)
         slope = keep.tile([P, PACK], F32)
         shift = keep.tile([P, PACK], F32)
-        scaled_parts = keep.tile([P, THIRDS], F32)
+        first_two = keep.tile([P, 1], F32)
+        first_total = keep.tile([P, 1], F32)
         w_head = keep.tile([P, HEAD], F32)
         ctx_grouped = keep.tile([P, CTX_COLS, PACK], BF16, align_bytes=64)
         ctx_codes = keep.tile([P, CTX_COLS], U32, align_bytes=64)
@@ -160,27 +161,31 @@ def tile_hierarchicalattention_pb_v_kernel(
                 op0=ALU.subtract, op1=ALU.mult, accum_out=sum_products[:, j : j + 1],
             )
 
-        def factors_on_scalar(j):
-            tok = slice(j, j + 1)
-            nc.scalar.activation(
-                out=slope[:, tok], in_=sum_products[:, tok], func=ACT.Identity, scale=neg_r2_mean[:, tok]
-            )
-            nc.scalar.activation(
-                out=shift[:, tok], in_=sum_products[:, tok], func=ACT.Identity,
-                scale=mu_r2_mean[:, tok], bias=neg_mean_ghr[:, tok],
+        def mean_of_ghr(j):
+            total = sum_ghr[:, j : j + 1]
+            if j == 0:
+                nc.gpsimd.tensor_tensor(
+                    out=first_two[:], in0=first_sums[:, 0:1], in1=first_sums[:, 1:2], op=ALU.add
+                )
+                nc.gpsimd.tensor_tensor(
+                    out=first_total[:], in0=first_two[:], in1=first_sums[:, 2:3], op=ALU.add
+                )
+                total = first_total[:]
+            nc.gpsimd.tensor_scalar(
+                out=neg_mean_ghr[:, j : j + 1], in0=total, scalar1=-1.0 / FEATURES, scalar2=None,
+                op0=ALU.mult,
             )
 
-        def mean_on_scalar(j):
-            if j == 0:
-                nc.scalar.activation(
-                    out=scaled_parts[:], in_=first_sums[:], func=ACT.Identity, scale=-1.0 / FEATURES,
-                    accum_out=neg_mean_ghr[:, 0:1],
-                )
-            else:
-                nc.scalar.activation(
-                    out=neg_mean_ghr[:, j : j + 1], in_=sum_ghr[:, j : j + 1], func=ACT.Identity,
-                    scale=-1.0 / FEATURES,
-                )
+        def slope_and_shift(j):
+            tok = slice(j, j + 1)
+            nc.gpsimd.tensor_scalar(
+                out=slope[:, tok], in0=sum_products[:, tok], scalar1=neg_r2_mean[:, tok],
+                scalar2=None, op0=ALU.mult,
+            )
+            nc.gpsimd.tensor_scalar(
+                out=shift[:, tok], in0=sum_products[:, tok], scalar1=mu_r2_mean[:, tok],
+                scalar2=neg_mean_ghr[:, tok], op0=ALU.mult, op1=ALU.add,
+            )
 
         def draw_line(j, c, lo=0):
             nc.scalar.activation(
@@ -195,8 +200,10 @@ def tile_hierarchicalattention_pb_v_kernel(
                 in_=ctx_raw[i][:].rearrange("p k j (c i) -> p k c j i", i=RUN),
             )
 
-        def quantise_ctx(n):
+        def quantise_ctx(n, part=None):
             cols = slice(n * N_TILE, (n + 1) * N_TILE)
+            if part is not None:
+                cols = slice(n * N_TILE + part * HALF_COLS, n * N_TILE + (part + 1) * HALF_COLS)
             nc.vector.quantize_mx(
                 out=ctx_codes[:, cols].bitcast(E4M3_X4),
                 scales=ctx_scales[:, cols],
@@ -242,51 +249,51 @@ def tile_hierarchicalattention_pb_v_kernel(
         )
         nc.gpsimd.tensor_tensor(out=mu_r2_mean[:], in0=r2_mean[:], in1=mu_sb[:], op=ALU.mult)
 
+        mean_of_ghr(0)
         sum_of_products(0)
+        slope_and_shift(0)
         scale_grad(1)
+        mean_of_ghr(1)
+        scale_grad(2)
+        mean_of_ghr(2)
+        sum_of_products(1)
+        slope_and_shift(1)
+        scale_grad(3)
+        mean_of_ghr(last)
+        sum_of_products(2)
+        slope_and_shift(2)
+        sum_of_products(last)
+        slope_and_shift(last)
+
         regroup_ctx(0)
         regroup_ctx(1)
-        mean_on_scalar(0)
-        factors_on_scalar(0)
         draw_line(0, 0)
-        sum_of_products(1)
-        scale_grad(2)
-        regroup_ctx(2)
-        mean_on_scalar(1)
-        factors_on_scalar(1)
-        draw_line(1, 0)
         draw_line(0, 1)
         draw_line(0, 2)
-        sum_of_products(2)
-        scale_grad(3)
+        regroup_ctx(2)
+        draw_line(1, 0)
         regroup_ctx(3)
         regroup_ctx(4)
-        mean_on_scalar(2)
-        factors_on_scalar(2)
-        draw_line(2, 0)
-        mean_on_scalar(last)
         nc.scalar.activation(
             out=w_head[:], in_=y_sb[last][:, 0:HEAD], func=ACT.Identity,
             bias=mu_r2_mean[:, last : last + 1], scale=neg_r2_mean[:, last : last + 1],
         )
-        regroup_ctx(5)
         draw_line(1, 1)
-        draw_line(1, 2)
-        quantise_ctx(0)
-        sum_of_products(last)
-        nc.vector.tensor_scalar(
-            out=line[0][:, last, 0:HEAD], in0=w_head[:], scalar1=sum_products[:, last : last + 1],
-            scalar2=neg_mean_ghr[:, last : last + 1], op0=ALU.mult, op1=ALU.add,
+        draw_line(2, 0)
+        nc.scalar.activation(
+            out=line[0][:, last, 0:HEAD], in_=w_head[:], func=ACT.Identity,
+            bias=neg_mean_ghr[:, last : last + 1], scale=sum_products[:, last : last + 1],
         )
-        factors_on_scalar(last)
+        regroup_ctx(5)
         draw_line(last, 0, HEAD)
-        draw_line(last - 1, 1)
+        draw_line(2, 1)
         draw_line(last, 1)
+        quantise_ctx(0)
 
         def draw_late(m):
             if m == 2 * TILES_PER_THIRD:
                 c = m // TILES_PER_THIRD
-                for j in (last - 1, last):
+                for j in (1, last - 1, last):
                     nc.vector.tensor_scalar(
                         out=line[c][:, j, :], in0=y_sb[j][:, c * N_TILE : (c + 1) * N_TILE],
                         scalar1=slope[:, j : j + 1], scalar2=shift[:, j : j + 1],
@@ -294,10 +301,11 @@ def tile_hierarchicalattention_pb_v_kernel(
                     )
 
         add_dy(0)
+        quantise_ctx(1, 0)
         quantise_dy(0)
-        quantise_ctx(1)
-        add_dy(1)
+        quantise_ctx(1, 1)
         quantise_ctx(2)
+        add_dy(1)
         quantise_dy(1)
         add_dy(2)
         for m in range(M_TILES):
@@ -324,7 +332,7 @@ def tile_hierarchicalattention_pb_v_kernel(
             result = results.tile([P, CTX_COLS], F32)
             for n in range(N_TILES):
                 cols = slice(n * N_TILE, (n + 1) * N_TILE)
-                if n == N_TILES - 1 and m > 3:
+                if (m * N_TILES + n) % 4 == 3 and m > 1:
                     nc.vector.tensor_copy(out=result[:, cols], in_=banks[n][:])
                 else:
                     nc.scalar.copy(out=result[:, cols], in_=banks[n][:])

@@ -109,10 +109,10 @@ def tile_hierarchicalattention_pb_v_kernel(
         load_y(1)
         load_ctx(2)
         load_g(3)
-        load_y(2)
         load_ctx(3)
-        load_ctx(4)
+        load_y(2)
         load_y(3)
+        load_ctx(4)
         load_ctx(5)
 
         gain_row = keep.tile([P, FEATURES], BF16)
@@ -131,15 +131,14 @@ def tile_hierarchicalattention_pb_v_kernel(
             gain_banks.append(gain_bank)
 
         ghr = keep.tile([P, PACK, FEATURES], F32)
-        products = keep.tile([P, FEATURES], F32)
+        products = [keep.tile([P, FEATURES], F32, name="products%d" % i) for i in range(2)]
         line = [keep.tile([P, PACK, N_TILE], F32, name="line%d" % c) for c in range(THIRDS)]
         sum_ghr = keep.tile([P, PACK], F32)
         sum_products = keep.tile([P, PACK], F32)
         neg_mean_ghr = keep.tile([P, PACK], F32)
         slope = keep.tile([P, PACK], F32)
         shift = keep.tile([P, PACK], F32)
-        first_two = keep.tile([P, 1], F32)
-        first_total = keep.tile([P, 1], F32)
+        scaled_parts = keep.tile([P, THIRDS], F32)
         w_head = keep.tile([P, HEAD], F32)
         ctx_grouped = keep.tile([P, CTX_COLS, PACK], BF16, align_bytes=64)
         ctx_codes = keep.tile([P, CTX_COLS], U32, align_bytes=64)
@@ -157,35 +156,31 @@ def tile_hierarchicalattention_pb_v_kernel(
 
         def sum_of_products(j):
             nc.vector.scalar_tensor_tensor(
-                out=products[:], in0=y_sb[j][:], scalar=mu_sb[:, j : j + 1], in1=ghr[:, j, :],
+                out=products[j % 2][:], in0=y_sb[j][:], scalar=mu_sb[:, j : j + 1], in1=ghr[:, j, :],
                 op0=ALU.subtract, op1=ALU.mult, accum_out=sum_products[:, j : j + 1],
             )
 
-        def mean_of_ghr(j):
-            total = sum_ghr[:, j : j + 1]
-            if j == 0:
-                nc.gpsimd.tensor_tensor(
-                    out=first_two[:], in0=first_sums[:, 0:1], in1=first_sums[:, 1:2], op=ALU.add
-                )
-                nc.gpsimd.tensor_tensor(
-                    out=first_total[:], in0=first_two[:], in1=first_sums[:, 2:3], op=ALU.add
-                )
-                total = first_total[:]
-            nc.gpsimd.tensor_scalar(
-                out=neg_mean_ghr[:, j : j + 1], in0=total, scalar1=-1.0 / FEATURES, scalar2=None,
-                op0=ALU.mult,
+        def factors_on_scalar(j):
+            tok = slice(j, j + 1)
+            nc.scalar.activation(
+                out=slope[:, tok], in_=sum_products[:, tok], func=ACT.Identity, scale=neg_r2_mean[:, tok]
+            )
+            nc.scalar.activation(
+                out=shift[:, tok], in_=sum_products[:, tok], func=ACT.Identity,
+                scale=mu_r2_mean[:, tok], bias=neg_mean_ghr[:, tok],
             )
 
-        def slope_and_shift(j):
-            tok = slice(j, j + 1)
-            nc.gpsimd.tensor_scalar(
-                out=slope[:, tok], in0=sum_products[:, tok], scalar1=neg_r2_mean[:, tok],
-                scalar2=None, op0=ALU.mult,
-            )
-            nc.gpsimd.tensor_scalar(
-                out=shift[:, tok], in0=sum_products[:, tok], scalar1=mu_r2_mean[:, tok],
-                scalar2=neg_mean_ghr[:, tok], op0=ALU.mult, op1=ALU.add,
-            )
+        def mean_on_scalar(j):
+            if j == 0:
+                nc.scalar.activation(
+                    out=scaled_parts[:], in_=first_sums[:], func=ACT.Identity, scale=-1.0 / FEATURES,
+                    accum_out=neg_mean_ghr[:, 0:1],
+                )
+            else:
+                nc.scalar.activation(
+                    out=neg_mean_ghr[:, j : j + 1], in_=sum_ghr[:, j : j + 1], func=ACT.Identity,
+                    scale=-1.0 / FEATURES,
+                )
 
         def draw_line(j, c, lo=0):
             nc.scalar.activation(
@@ -249,42 +244,43 @@ def tile_hierarchicalattention_pb_v_kernel(
         )
         nc.gpsimd.tensor_tensor(out=mu_r2_mean[:], in0=r2_mean[:], in1=mu_sb[:], op=ALU.mult)
 
-        mean_of_ghr(0)
         sum_of_products(0)
-        slope_and_shift(0)
         scale_grad(1)
-        mean_of_ghr(1)
         scale_grad(2)
-        mean_of_ghr(2)
         sum_of_products(1)
-        slope_and_shift(1)
         scale_grad(3)
-        mean_of_ghr(last)
         sum_of_products(2)
-        slope_and_shift(2)
         sum_of_products(last)
-        slope_and_shift(last)
 
         regroup_ctx(0)
         regroup_ctx(1)
+        mean_on_scalar(0)
+        factors_on_scalar(0)
         draw_line(0, 0)
         draw_line(0, 1)
         draw_line(0, 2)
         regroup_ctx(2)
-        draw_line(1, 0)
         regroup_ctx(3)
-        regroup_ctx(4)
+        mean_on_scalar(1)
+        factors_on_scalar(1)
+        draw_line(1, 0)
+        draw_line(1, 1)
+        draw_line(1, 2)
+        mean_on_scalar(2)
+        mean_on_scalar(last)
         nc.scalar.activation(
             out=w_head[:], in_=y_sb[last][:, 0:HEAD], func=ACT.Identity,
             bias=mu_r2_mean[:, last : last + 1], scale=neg_r2_mean[:, last : last + 1],
         )
-        draw_line(1, 1)
+        regroup_ctx(4)
+        factors_on_scalar(2)
         draw_line(2, 0)
         nc.scalar.activation(
             out=line[0][:, last, 0:HEAD], in_=w_head[:], func=ACT.Identity,
             bias=neg_mean_ghr[:, last : last + 1], scale=sum_products[:, last : last + 1],
         )
         regroup_ctx(5)
+        factors_on_scalar(last)
         draw_line(last, 0, HEAD)
         draw_line(2, 1)
         draw_line(last, 1)
@@ -293,7 +289,7 @@ def tile_hierarchicalattention_pb_v_kernel(
         def draw_late(m):
             if m == 2 * TILES_PER_THIRD:
                 c = m // TILES_PER_THIRD
-                for j in (1, last - 1, last):
+                for j in (last - 1, last):
                     nc.vector.tensor_scalar(
                         out=line[c][:, j, :], in0=y_sb[j][:, c * N_TILE : (c + 1) * N_TILE],
                         scalar1=slope[:, j : j + 1], scalar2=shift[:, j : j + 1],

from contextlib import ExitStack

import concourse.mybir as mybir

F32 = mybir.dt.float32
BF16 = mybir.dt.bfloat16
U32 = mybir.dt.uint32
U8 = mybir.dt.uint8
E4M3_X4 = mybir.dt.float8_e4m3fn_x4
E5M2_X4 = mybir.dt.float8_e5m2_x4
ALU = mybir.AluOpType
ACT = mybir.ActivationFunctionType

P = 128
PACK = 4
BATCH = 4
HEADS = 12
SEQ = 128
HEAD_DIM = 128
FEATURES = 1536
CTX_COLS = HEADS * HEAD_DIM
M_TILE = 128
N_TILE = 512
M_TILES = FEATURES // M_TILE
N_TILES = CTX_COLS // N_TILE
HEADS_PER_N_TILE = N_TILE // HEAD_DIM
RUN = 4

FLOPS = 2 * BATCH * SEQ * FEATURES * CTX_COLS
BYTES = (
    2 * BATCH * SEQ * CTX_COLS
    + 2 * BATCH * SEQ * FEATURES
    + 4 * BATCH * SEQ * FEATURES
    + 2 * FEATURES
    + 2 * 4 * BATCH * SEQ
    + 4 * FEATURES * CTX_COLS
)


def by_slot(planes):
    return planes.rearrange("p j (c i) -> p c j i", i=RUN)


def by_column(grouped):
    return grouped.rearrange("p (c i) j -> p c j i", i=RUN)


def slots_of(x):
    return x.rearrange("b (q j) h -> j q b h", j=PACK)


def tile_hierarchicalattention_pb_v_kernel(
    tc, ctx_heads, Wo, bo, features, ln_g, ln_b, y, mu, rstd, grad_out, out
):
    nc = tc.nc
    assert BATCH == PACK and SEQ == P
    THIRDS = FEATURES // N_TILE
    HALF = 2
    HALVES = HEADS // HALF
    HALF_COLS = HALF * HEAD_DIM
    TILES_PER_THIRD = N_TILE // M_TILE
    HEAD = 2 * M_TILE

    with ExitStack() as stack:
        keep = stack.enter_context(tc.tile_pool(name="keep", bufs=1))
        results = stack.enter_context(tc.tile_pool(name="results", bufs=4))
        psum = stack.enter_context(tc.psum_pool(name="psum", bufs=8))
        stack.enter_context(tc.manual_schedule())

        ln_g_sb = keep.tile([1, FEATURES], BF16)
        nc.sync.dma_start(out=ln_g_sb[:], in_=ln_g.rearrange("(o h) -> o h", o=1))
        rstd_sb = keep.tile([P, PACK], F32)
        mu_sb = keep.tile([P, PACK], F32)
        nc.sync.dma_start(out=rstd_sb[:], in_=rstd.rearrange("b (q j) o -> q b (j o)", j=PACK))

        g_first = [keep.tile([P, N_TILE], BF16, name="g_first%d" % n) for n in range(THIRDS)]
        g_sb = [keep.tile([P, FEATURES], BF16, name="g_sb%d" % j) for j in range(1, PACK)]
        y_sb = [keep.tile([P, FEATURES], F32, name="y_sb%d" % j) for j in range(PACK)]
        ctx_raw = [
            keep.tile([P, HALF, PACK, HEAD_DIM], BF16, name="ctx_raw%d" % i) for i in range(HALVES)
        ]

        def load_g(j):
            if j == 0:
                for n in range(THIRDS):
                    nc.sync.dma_start(
                        out=g_first[n][:], in_=slots_of(grad_out)[0][:, :, n * N_TILE : (n + 1) * N_TILE]
                    )
            else:
                nc.sync.dma_start(out=g_sb[j - 1][:], in_=slots_of(grad_out)[j])

        def load_y(j):
            nc.sync.dma_start(out=y_sb[j][:], in_=slots_of(y)[j])

        def load_ctx(i):
            for k in range(HALF):
                nc.sync.dma_start(
                    out=ctx_raw[i][:, k, :, :].rearrange("p j d -> p (j d)"),
                    in_=ctx_heads[:, i * HALF + k].rearrange("b (q j) d -> q b (j d)", j=PACK),
                )

        load_g(0)
        nc.sync.dma_start(out=mu_sb[:], in_=mu.rearrange("b (q j) o -> q b (j o)", j=PACK))
        load_y(0)
        load_ctx(0)
        load_g(1)
        load_ctx(1)
        load_g(2)
        load_y(1)
        load_ctx(2)
        load_g(3)
        load_ctx(3)
        load_y(2)
        load_y(3)
        load_ctx(4)
        load_ctx(5)

        gain_row = keep.tile([P, FEATURES], BF16)
        nc.vector.memset(gain_row[:], 0.0)
        ones = keep.tile([P, P], BF16)
        nc.vector.memset(ones[:], 1.0)
        gain = keep.tile([P, FEATURES], BF16)
        gain_banks = []
        for n in range(THIRDS):
            cols = slice(n * N_TILE, (n + 1) * N_TILE)
            nc.vector.tensor_copy(out=gain_row[0:1, cols], in_=ln_g_sb[:, cols])
            gain_bank = psum.tile([P, N_TILE], BF16, tag="bank")
            nc.tensor.matmul(
                out=gain_bank[:], lhsT=ones[:], rhs=gain_row[:, cols], start=True, stop=True
            )
            gain_banks.append(gain_bank)

        ghr = keep.tile([P, PACK, FEATURES], F32)
        products = [keep.tile([P, FEATURES], F32, name="products%d" % i) for i in range(2)]
        line = [keep.tile([P, PACK, N_TILE], F32, name="line%d" % c) for c in range(THIRDS)]
        sum_ghr = keep.tile([P, PACK], F32)
        sum_products = keep.tile([P, PACK], F32)
        neg_mean_ghr = keep.tile([P, PACK], F32)
        slope = keep.tile([P, PACK], F32)
        shift = keep.tile([P, PACK], F32)
        scaled_parts = keep.tile([P, THIRDS], F32)
        w_head = keep.tile([P, HEAD], F32)
        ctx_grouped = keep.tile([P, CTX_COLS, PACK], BF16, align_bytes=64)
        ctx_codes = keep.tile([P, CTX_COLS], U32, align_bytes=64)
        ctx_scales = keep.tile([P, CTX_COLS], U8, align_bytes=64)
        dy_grouped = keep.tile([P, FEATURES, PACK], BF16, align_bytes=64)
        dy_codes = keep.tile([P, FEATURES], U32, align_bytes=64)
        dy_scales = keep.tile([P, FEATURES], U8, align_bytes=64)
        last = PACK - 1

        def scale_grad(j):
            nc.vector.scalar_tensor_tensor(
                out=ghr[:, j, :], in0=gain[:], scalar=rstd_sb[:, j : j + 1], in1=g_sb[j - 1][:],
                op0=ALU.mult, op1=ALU.mult, accum_out=sum_ghr[:, j : j + 1],
            )

        def sum_of_products(j):
            nc.vector.scalar_tensor_tensor(
                out=products[j % 2][:], in0=y_sb[j][:], scalar=mu_sb[:, j : j + 1], in1=ghr[:, j, :],
                op0=ALU.subtract, op1=ALU.mult, accum_out=sum_products[:, j : j + 1],
            )

        def factors_on_scalar(j):
            tok = slice(j, j + 1)
            nc.scalar.activation(
                out=slope[:, tok], in_=sum_products[:, tok], func=ACT.Identity, scale=neg_r2_mean[:, tok]
            )
            nc.scalar.activation(
                out=shift[:, tok], in_=sum_products[:, tok], func=ACT.Identity,
                scale=mu_r2_mean[:, tok], bias=neg_mean_ghr[:, tok],
            )

        def mean_on_scalar(j):
            if j == 0:
                nc.scalar.activation(
                    out=scaled_parts[:], in_=first_sums[:], func=ACT.Identity, scale=-1.0 / FEATURES,
                    accum_out=neg_mean_ghr[:, 0:1],
                )
            else:
                nc.scalar.activation(
                    out=neg_mean_ghr[:, j : j + 1], in_=sum_ghr[:, j : j + 1], func=ACT.Identity,
                    scale=-1.0 / FEATURES,
                )

        def draw_line(j, c, lo=0):
            nc.scalar.activation(
                out=line[c][:, j, lo:N_TILE], in_=y_sb[j][:, c * N_TILE + lo : (c + 1) * N_TILE],
                func=ACT.Identity, bias=shift[:, j : j + 1], scale=slope[:, j : j + 1],
            )

        def regroup_ctx(i):
            cols = slice(i * HALF_COLS, (i + 1) * HALF_COLS)
            nc.scalar.copy(
                out=ctx_grouped[:, cols, :].rearrange("p (k c i) j -> p k c j i", k=HALF, i=RUN),
                in_=ctx_raw[i][:].rearrange("p k j (c i) -> p k c j i", i=RUN),
            )

        def quantise_ctx(n, part=None):
            cols = slice(n * N_TILE, (n + 1) * N_TILE)
            if part is not None:
                cols = slice(n * N_TILE + part * HALF_COLS, n * N_TILE + (part + 1) * HALF_COLS)
            nc.vector.quantize_mx(
                out=ctx_codes[:, cols].bitcast(E4M3_X4),
                scales=ctx_scales[:, cols],
                in_=ctx_grouped[:, cols, :].rearrange("p w b -> p (w b)"),
            )

        def add_dy(m):
            rows = slice(m * M_TILE, (m + 1) * M_TILE)
            in_third = slice((m % TILES_PER_THIRD) * M_TILE, (m % TILES_PER_THIRD + 1) * M_TILE)
            nc.vector.tensor_tensor(
                out=by_column(dy_grouped[:, rows, :]),
                in0=by_slot(ghr[:, :, rows]),
                in1=by_slot(line[m // TILES_PER_THIRD][:, :, in_third]),
                op=ALU.add,
            )

        def quantise_dy(m):
            rows = slice(m * M_TILE, (m + 1) * M_TILE)
            nc.vector.quantize_mx(
                out=dy_codes[:, rows].bitcast(E5M2_X4),
                scales=dy_scales[:, rows],
                in_=dy_grouped[:, rows, :].rearrange("p w b -> p (w b)"),
            )

        first_sums = keep.tile([P, THIRDS], F32)
        for n in range(THIRDS):
            cols = slice(n * N_TILE, (n + 1) * N_TILE)
            nc.vector.scalar_tensor_tensor(
                out=ghr[:, 0, cols], in0=gain_banks[n][:], scalar=rstd_sb[:, 0:1],
                in1=g_first[n][:], op0=ALU.mult, op1=ALU.mult, accum_out=first_sums[:, n : n + 1],
            )
            nc.scalar.copy(out=gain[:, cols], in_=gain_banks[n][:])
        r2 = keep.tile([P, PACK], F32)
        r2_mean = keep.tile([P, PACK], F32)
        neg_r2_mean = keep.tile([P, PACK], F32)
        mu_r2_mean = keep.tile([P, PACK], F32)
        nc.gpsimd.tensor_tensor(out=r2[:], in0=rstd_sb[:], in1=rstd_sb[:], op=ALU.mult)
        nc.gpsimd.tensor_scalar(
            out=r2_mean[:], in0=r2[:], scalar1=1.0 / FEATURES, scalar2=None, op0=ALU.mult
        )
        nc.gpsimd.tensor_scalar(
            out=neg_r2_mean[:], in0=r2_mean[:], scalar1=-1.0, scalar2=None, op0=ALU.mult
        )
        nc.gpsimd.tensor_tensor(out=mu_r2_mean[:], in0=r2_mean[:], in1=mu_sb[:], op=ALU.mult)

        sum_of_products(0)
        scale_grad(1)
        scale_grad(2)
        sum_of_products(1)
        scale_grad(3)
        sum_of_products(2)
        sum_of_products(last)

        regroup_ctx(0)
        regroup_ctx(1)
        mean_on_scalar(0)
        factors_on_scalar(0)
        draw_line(0, 0)
        draw_line(0, 1)
        draw_line(0, 2)
        regroup_ctx(2)
        regroup_ctx(3)
        mean_on_scalar(1)
        factors_on_scalar(1)
        draw_line(1, 0)
        draw_line(1, 1)
        draw_line(1, 2)
        mean_on_scalar(2)
        mean_on_scalar(last)
        nc.scalar.activation(
            out=w_head[:], in_=y_sb[last][:, 0:HEAD], func=ACT.Identity,
            bias=mu_r2_mean[:, last : last + 1], scale=neg_r2_mean[:, last : last + 1],
        )
        regroup_ctx(4)
        factors_on_scalar(2)
        draw_line(2, 0)
        nc.scalar.activation(
            out=line[0][:, last, 0:HEAD], in_=w_head[:], func=ACT.Identity,
            bias=neg_mean_ghr[:, last : last + 1], scale=sum_products[:, last : last + 1],
        )
        regroup_ctx(5)
        factors_on_scalar(last)
        draw_line(last, 0, HEAD)
        draw_line(2, 1)
        draw_line(last, 1)
        quantise_ctx(0)

        def draw_late(m):
            if m == 2 * TILES_PER_THIRD:
                c = m // TILES_PER_THIRD
                for j in (last - 1, last):
                    nc.vector.tensor_scalar(
                        out=line[c][:, j, :], in0=y_sb[j][:, c * N_TILE : (c + 1) * N_TILE],
                        scalar1=slope[:, j : j + 1], scalar2=shift[:, j : j + 1],
                        op0=ALU.mult, op1=ALU.add,
                    )

        add_dy(0)
        quantise_ctx(1, 0)
        quantise_dy(0)
        quantise_ctx(1, 1)
        quantise_ctx(2)
        add_dy(1)
        quantise_dy(1)
        add_dy(2)
        for m in range(M_TILES):
            rows = slice(m * M_TILE, (m + 1) * M_TILE)
            banks = []
            for n in range(N_TILES):
                cols = slice(n * N_TILE, (n + 1) * N_TILE)
                bank = psum.tile([P, N_TILE], F32, tag="bank")
                nc.tensor.matmul_mx(
                    out=bank[:],
                    lhsT=dy_codes[:, rows].bitcast(E5M2_X4),
                    lhsT_scale=dy_scales[:, rows],
                    rhs=ctx_codes[:, cols].bitcast(E4M3_X4),
                    rhs_scale=ctx_scales[:, cols],
                    start=True,
                    stop=True,
                )
                banks.append(bank)
            draw_late(m + 4)
            if m + 2 < M_TILES:
                quantise_dy(m + 2)
            if m + 3 < M_TILES:
                add_dy(m + 3)
            result = results.tile([P, CTX_COLS], F32)
            for n in range(N_TILES):
                cols = slice(n * N_TILE, (n + 1) * N_TILE)
                if (m * N_TILES + n) % 4 == 3 and m > 1:
                    nc.vector.tensor_copy(out=result[:, cols], in_=banks[n][:])
                else:
                    nc.scalar.copy(out=result[:, cols], in_=banks[n][:])
                if m <= 3:
                    nc.sync.dma_start(out=out[rows, cols], in_=result[:, cols])
            if m > 3:
                nc.sync.dma_start(out=out[rows, :], in_=result[:])
